import numpy as np
import ml_dtypes


def mxq(x, axis, fmt="e4m3"):
    dtype, down = {"e4m3": (ml_dtypes.float8_e4m3fn, 7), "e5m2": (ml_dtypes.float8_e5m2, 14)}[fmt]
    v = np.moveaxis(np.asarray(x, np.float32).astype(ml_dtypes.bfloat16).astype(np.float64), axis, -1)
    blocks = v.reshape(v.shape[:-1] + (-1, 32))
    amax = np.abs(blocks).max(-1, keepdims=True)
    byte = np.maximum(np.where(amax > 0, np.frexp(amax)[1] - 1 + 127, 0) - down, 1)
    scale = np.exp2(byte - 127.0)
    codes = (blocks / scale).astype(np.float32).astype(dtype).astype(np.float64)
    return np.moveaxis((codes * scale).reshape(v.shape), -1, axis)


WIDE = False


def mx_kscale(k):
    if not WIDE:
        return np.ones(k)
    levels = np.array([10, -10, 5, -5, 0])
    if k % 512:
        return np.exp2(np.random.permutation(np.resize(levels, k // 32))).repeat(32)
    a = np.empty((k // 512, 16))
    for p in range(k // 512):
        a[p, :8] = np.random.permutation(np.resize(levels, 8))
        for g in range(8):
            far = levels[np.abs(levels - a[p, g]) >= 10]
            a[p, g + 8] = far[np.random.randint(len(far))]
    return np.exp2(a.ravel()).repeat(32)


BF16 = ml_dtypes.bfloat16


def bf(x):
    return np.asarray(x, np.float32).astype(BF16)


def f64(x):
    return np.asarray(x).astype(np.float64)


B, T, N, D, H, F = 2, 512, 4, 512, 8, 1024
S = B * N
EPS = 1e-5


def layernorm(v, g, b):
    mu = v.mean(-1, keepdims=True)
    var = np.square(v - mu).mean(-1, keepdims=True)
    return (v - mu) / np.sqrt(var + EPS) * g + b


def draw0():
    s = mx_kscale(D)
    t = mx_kscale(D)
    return {"ax_cat": bf(np.random.standard_normal((S, T, D)) * 4.0 * s),
            "features": bf(np.random.standard_normal((B, T, N, D))),
            "wout_w": bf(np.random.standard_normal((D, D)) * 0.5 / np.sqrt(D) / s),
            "ln_g": bf((1.0 + 0.1 * np.random.standard_normal(D)) * t),
            "ln_b": bf(0.1 * np.random.standard_normal(D) * t),
            "ff1_w": bf(np.random.standard_normal((F, D)) / np.sqrt(D) / t),
            "ff1_b": bf(0.1 * np.random.standard_normal(F))}


def core(ax_cat, features, wout_w, ln_g, ln_b, ff1_w, ff1_b):
    x = f64(features).transpose(0, 2, 1, 3).reshape(S, T, D)
    y = mxq(f64(ax_cat), 2, "e4m3") @ mxq(f64(wout_w), 1, "e4m3").T
    m = layernorm(y + x, f64(ln_g), f64(ln_b))
    return np.maximum((mxq(m, 2, "e4m3") @ mxq(f64(ff1_w), 1, "e4m3").T) + f64(ff1_b), 0.0)


def e4m3fn_bytes(y):
    return np.clip(np.asarray(y, np.float64), -448.0, 448.0).astype(np.float32).astype(ml_dtypes.float8_e4m3fn).view(np.uint8)


def e4m3fn_values(b):
    return np.asarray(b, np.uint8).view(ml_dtypes.float8_e4m3fn).astype(np.float64)


def setup_inputs():
    d = draw0()
    x0 = np.asarray(d['ax_cat']).astype(np.float64)
    s = (np.max(np.abs(x0), axis=(0, 1), keepdims=True) / 448.0).astype(np.float32)
    out = {}
    for k, v in d.items():
        if k == 'ax_cat':
            out['ax_cat_bytes'] = e4m3fn_bytes(x0 / s.astype(np.float64))
            out['ax_cat_scale'] = s
        else:
            out[k] = v
    return out


def reference(ax_cat_bytes, ax_cat_scale, features, wout_w, ln_g, ln_b, ff1_w, ff1_b):
    return core(e4m3fn_values(ax_cat_bytes) * ax_cat_scale.astype(np.float64), features, wout_w, ln_g, ln_b, ff1_w, ff1_b)

@@ -1,0 +1,310 @@
+from contextlib import ExitStack
+
+import concourse.mybir as mybir
+from concourse.masks import make_identity
+
+B, T, N, D, F = 2, 512, 4, 512, 1024
+S = B * N
+EPS = 1e-5
+FLOPS = 2 * S * T * D * (D + F)
+
+F32 = mybir.dt.float32
+BF16 = mybir.dt.bfloat16
+U32 = mybir.dt.uint32
+U8 = mybir.dt.uint8
+FP8 = mybir.dt.float8_e4m3fn
+FP8X4 = mybir.dt.float8_e4m3fn_x4
+ALU = mybir.AluOpType
+ACT = mybir.ActivationFunctionType
+
+P = 128
+PACK = 4
+BANK = 512
+TILES_PER_SEQ = T // P
+PAIRS = S * TILES_PER_SEQ // 2
+HEAD_PAIRS = 0
+TAIL_PAIRS = 2
+SCALAR_RELU_PAIRS = 1
+W1_BANKS = {1: (0, 1), 2: (2, 3)}
+W1_QUANT = (2, 3)
+GP_NORM_FROM = 0
+GP_NORM_TO = 14
+SHARED_RELU_PAIRS = 3
+FILL = 5
+F32_MAX = 3.4028234663852886e38
+
+
+def tile_temporalatt_pb_t_kernel(tc, ax_bytes, ax_scale, features, wout_w, ln_g, ln_b, ff1_w, ff1_b, out):
+    nc = tc.nc
+    with ExitStack() as ctx:
+        keep = ctx.enter_context(tc.tile_pool(name="keep", bufs=1))
+        work = ctx.enter_context(tc.tile_pool(name="work", bufs=3))
+        psum = ctx.enter_context(tc.psum_pool(name="psum", bufs=1))
+        ctx.enter_context(tc.manual_schedule())
+
+        ident = keep.tile([P, P], F32, name="ident")
+        make_identity(nc, ident[:])
+
+        ax_raw = {}
+        x_raw = {}
+
+        def pair_rows(seq_rows, k):
+            first = 2 * (k % 2)
+            return seq_rows.rearrange("(p j) d -> p j d", j=TILES_PER_SEQ)[:, first:first + 2, :]
+
+        def load_ax(k):
+            codes_in = keep.tile([P, 2, D], U8, name="ax_bytes_%d" % k)
+            nc.sync.dma_start(out=codes_in[:], in_=pair_rows(ax_bytes[k // 2], k))
+            ax_raw[k] = codes_in
+
+        def load_x(k):
+            s = k // 2
+            rows = keep.tile([P, 2, D], BF16, name="x_%d" % k)
+            nc.sync.dma_start(out=rows[:], in_=pair_rows(features[s // N, :, s % N, :], k))
+            x_raw[k] = rows
+
+        scale_col = keep.tile([P, PACK], F32, name="scale_col")
+        nc.sync.dma_start(out=scale_col[:], in_=ax_scale.rearrange("a b (p t) -> p (a b t)", t=PACK))
+        g_raw = keep.tile([P, PACK], BF16, name="g_raw")
+        nc.sync.dma_start(out=g_raw[:], in_=ln_g.rearrange("(p t) -> p t", t=PACK))
+        load_ax(0)
+        wo_raw = []
+        for half in range(2):
+            rows = keep.tile([P, 2, D], BF16, name="wo_raw_%d" % half)
+            nc.sync.dma_start(out=rows[:], in_=wout_w.rearrange("(m t) k -> m t k", t=PACK)[:, 2 * half:2 * half + 2, :])
+            wo_raw.append(rows)
+        load_ax(1)
+        load_x(0)
+        w1_raw = []
+        for half in range(2):
+            rows = keep.tile([P, PACK, D], BF16, name="w1_raw_%d" % half)
+            nc.sync.dma_start(out=rows[:], in_=ff1_w[half * BANK:(half + 1) * BANK, :].rearrange("(c m) k -> m c k", m=P))
+            w1_raw.append(rows)
+            load_ax(2 + half)
+            load_x(1 + half)
+        b_raw = keep.tile([P, PACK], BF16, name="b_raw")
+        nc.sync.dma_start(out=b_raw[:], in_=ln_b.rearrange("(p t) -> p t", t=PACK))
+        load_ax(4)
+        bias_rows = keep.tile([P, F], BF16, name="bias_rows")
+        nc.sync.dma_start(out=bias_rows[:], in_=ff1_b.partition_broadcast(P))
+        for k in range(3, PAIRS):
+            load_x(k)
+            if k + 2 < PAIRS:
+                load_ax(k + 2)
+
+        g_col = keep.tile([P, PACK], F32, name="g_col")
+        nc.scalar.activation(out=g_col[:], in_=g_raw[:], func=ACT.Copy)
+        b_col = keep.tile([P, PACK], F32, name="b_col")
+
+        scale_rows = psum.tile([P, P, PACK], F32, name="scale_rows")
+        for t in range(PACK):
+            nc.tensor.transpose(scale_rows[:, :, t], scale_col[:, t:t + 1].to_broadcast([P, P]), ident[:])
+
+        def turn_weight_rows(raw, grouped, c0):
+            bank = psum.tile([P, 2, 2, P], F32, name="weight_bank", tag="acc", bufs=4)
+            for c in range(2):
+                words = raw[:, c, :].bitcast(F32)
+                for u in range(2):
+                    nc.tensor.transpose(bank[:, c, u, :], words[:, u::2], ident[:])
+            dst = grouped[:, c0 * P * PACK:(c0 + 2) * P * PACK].bitcast(F32)
+            nc.scalar.copy(out=dst.rearrange("p (c m u) -> p c m u", c=2, u=2), in_=bank[:].rearrange("p c u m -> p c m u"))
+
+        def quantize(grouped, codes, scales):
+            nc.vector.quantize_mx(out=codes[:].bitcast(FP8X4), scales=scales[:], in_=grouped[:])
+
+        def weight_tiles(name):
+            grouped = keep.tile([P, BANK * PACK], BF16, name=name + "_grouped", align_bytes=64)
+            codes = keep.tile([P, BANK], U32, name=name + "_codes", align_bytes=64)
+            scales = keep.tile([P, BANK], U8, name=name + "_scales", align_bytes=64)
+            return grouped, codes, scales
+
+        wo = weight_tiles("wo")
+        w1 = [weight_tiles("w1_0"), weight_tiles("w1_1")]
+
+        ax_scaled, ax_bank, ax_grouped, ax_q = {}, {}, {}, {}
+        acc, resid, sums, sumsq, std, rstd, shift = {}, {}, {}, {}, {}, {}, {}
+        normed, z_banks, planes, m_grouped, m_q, staged = {}, {}, {}, {}, {}, {}
+
+        def scale_ax(k, j):
+            if j == 0:
+                ax_scaled[k] = work.tile([P, 2, D], BF16, name="ax_scaled")
+            nc.vector.tensor_tensor(out=ax_scaled[k][:, j, :], in0=ax_raw[k][:, j, :].bitcast(FP8),
+                                    in1=scale_rows[:].rearrange("m p t -> m (p t)"), op=ALU.mult)
+
+        def turn_ax(k):
+            ax_bank[k] = psum.tile([P, 2, 2, P], F32, name="ax_bank")
+            for j in range(2):
+                words = ax_scaled[k][:, j, :].bitcast(F32)
+                for u in range(2):
+                    nc.tensor.transpose(ax_bank[k][:, j, u, :], words[:, u::2], ident[:])
+
+        def group_ax(k):
+            ax_grouped[k] = work.tile([P, 2 * P * PACK], BF16, name="ax_grouped", align_bytes=64)
+            nc.scalar.copy(out=ax_grouped[k][:].bitcast(F32).rearrange("p (j r u) -> p j r u", j=2, u=2),
+                           in_=ax_bank[k][:].rearrange("p j u r -> p j r u"))
+
+        def quantize_pair(grouped, name):
+            codes = work.tile([P, 2 * P], U32, name=name + "_codes", align_bytes=64)
+            scales = work.tile([P, 2 * P], U8, name=name + "_scales", align_bytes=64)
+            quantize(grouped, codes, scales)
+            return codes, scales
+
+        def matmul(key, operand, j, weight):
+            codes, scales = operand
+            acc[key] = psum.tile([P, BANK], F32, name="acc", bufs=4)
+            rows = slice(j * P, (j + 1) * P)
+            nc.tensor.matmul_mx(out=acc[key][:], lhsT=codes[:, rows].bitcast(FP8X4), lhsT_scale=scales[:, rows],
+                                rhs=weight[1][:].bitcast(FP8X4), rhs_scale=weight[2][:], start=True, stop=True)
+
+        def add_residual(k, j):
+            if j == 0:
+                sums[k] = work.tile([P, 2], F32, name="sums", bufs=4)
+                sumsq[k] = work.tile([P, 2], F32, name="sumsq", bufs=4)
+            resid[k, j] = work.tile([P, D], F32, name="resid", bufs=8)
+            nc.vector.scalar_tensor_tensor(
+                out=resid[k, j][:].rearrange("p (t m) -> p t m", t=PACK),
+                in0=acc["proj", k, j][:].rearrange("p (t m) -> p t m", t=PACK), scalar=1.0,
+                in1=x_raw[k][:, j, :].rearrange("p (m t) -> p t m", t=PACK),
+                op0=ALU.mult, op1=ALU.add, accum_out=sums[k][:, j:j + 1])
+
+        def square_sum(k, j):
+            squares = work.tile([P, D], BF16, name="squares", bufs=2)
+            nc.scalar.activation(out=squares[:], in_=resid[k, j][:], func=ACT.Square, scale=-float(D),
+                                 bias=sums[k][:, j:j + 1], accum_out=sumsq[k][:, j:j + 1])
+
+        def std_of(k):
+            std[k] = work.tile([P, 2], F32, name="std")
+            nc.scalar.activation(out=std[k][:], in_=sumsq[k][:], func=ACT.Sqrt, scale=1.0 / D ** 3, bias=EPS)
+
+        def rstd_of(k):
+            rstd[k] = work.tile([P, 2], F32, name="rstd")
+            nc.vector.reciprocal(out=rstd[k][:], in_=std[k][:])
+
+        def shift_of(k):
+            shift[k] = work.tile([P, 2], F32, name="shift")
+            nc.vector.scalar_tensor_tensor(out=shift[k][:], in0=sums[k][:], scalar=-1.0 / D, in1=rstd[k][:],
+                                           op0=ALU.mult, op1=ALU.mult)
+
+        def normalise(k):
+            for j in range(2):
+                normed[k, j] = work.tile([P, D], F32, name="normed", bufs=4)
+                if GP_NORM_FROM <= k < GP_NORM_TO:
+                    nc.gpsimd.tensor_scalar(out=normed[k, j][:], in0=resid[k, j][:], scalar1=rstd[k][:, j:j + 1],
+                                            scalar2=shift[k][:, j:j + 1], op0=ALU.mult, op1=ALU.add)
+                else:
+                    nc.scalar.activation(out=normed[k, j][:], in_=resid[k, j][:], func=ACT.Identity,
+                                         scale=rstd[k][:, j:j + 1], bias=shift[k][:, j:j + 1])
+
+        def turn_normed(k, j):
+            if j == 0:
+                for h in range(2):
+                    z_banks[k, h] = psum.tile([P, 2, 2 * P], F32, name="z_bank", bufs=2)
+            for t in range(PACK):
+                nc.tensor.transpose(z_banks[k, t // 2][:, t % 2, j * P:(j + 1) * P], normed[k, j][:, t * P:(t + 1) * P], ident[:])
+
+        def gain_and_bias(k):
+            planes[k] = work.tile([P, PACK, 2 * P], BF16, name="planes", bufs=2)
+            for t in range(PACK):
+                nc.scalar.activation(out=planes[k][:, t, :], in_=z_banks[k, t // 2][:, t % 2, :], func=ACT.Identity,
+                                     scale=g_col[:, t:t + 1], bias=b_col[:, t:t + 1])
+
+        def vector_groups(k):
+            return k < HEAD_PAIRS or k >= PAIRS - TAIL_PAIRS
+
+        def group_m(k):
+            m_grouped[k] = work.tile([P, 2 * P * PACK], BF16, name="m_grouped", align_bytes=64)
+            copy = nc.vector.tensor_copy if vector_groups(k) else nc.scalar.copy
+            copy(out=m_grouped[k][:].rearrange("p (c i t) -> p c t i", i=4, t=PACK),
+                 in_=planes[k][:].rearrange("p t (c i) -> p c t i", i=4))
+
+        def add_bias(k, j, half):
+            if half == 0:
+                staged[k, j] = work.tile([P, F], F32, name="staged", bufs=6)
+            cols = slice(half * BANK, (half + 1) * BANK)
+            nc.vector.tensor_tensor(out=staged[k, j][:, cols], in0=acc["ff", k, j, half][:], in1=bias_rows[:, cols], op=ALU.add)
+            rows = out[k // 2].rearrange("(p j) f -> p j f", j=TILES_PER_SEQ)[:, 2 * (k % 2) + j, :]
+            if k >= PAIRS - SCALAR_RELU_PAIRS or (j == 0 and k >= PAIRS - SHARED_RELU_PAIRS):
+                nc.scalar.activation(out=staged[k, j][:, cols], in_=staged[k, j][:, cols], func=ACT.Relu)
+                nc.sync.dma_start(out=rows[:, cols], in_=staged[k, j][:, cols])
+            elif half == 1:
+                nc.gpsimd.tensor_scalar(out=staged[k, j][:], in0=staged[k, j][:], scalar1=F32_MAX, scalar2=0.0,
+                                        op0=ALU.min, op1=ALU.max)
+                nc.sync.dma_start(out=rows, in_=staged[k, j][:])
+
+        def ff_matmul(k, j, half):
+            matmul(("ff", k, j, half), m_q[k], j, w1[half])
+
+        def proj_matmul(k, j):
+            matmul(("proj", k, j), ax_q[k], j, wo)
+
+        def live(k):
+            return 0 <= k < PAIRS
+
+        turn_weight_rows(wo_raw[0], wo[0], 0)
+        turn_weight_rows(wo_raw[1], wo[0], 2)
+
+        for n in range(PAIRS + 7):
+            filling = n < FILL
+            if n == 2:
+                nc.scalar.activation(out=b_col[:], in_=b_raw[:], func=ACT.Copy)
+            if live(n - 1) and filling:
+                proj_matmul(n - 1, 0)
+                proj_matmul(n - 1, 1)
+            if live(n - 2):
+                square_sum(n - 2, 0)
+                square_sum(n - 2, 1)
+            if live(n - 4) and not vector_groups(n - 4):
+                group_m(n - 4)
+            if live(n - 2):
+                std_of(n - 2)
+            if live(n - 3):
+                normalise(n - 3)
+            if live(n - 3) and not filling:
+                turn_normed(n - 3, 0)
+            if live(n):
+                scale_ax(n, 0)
+                scale_ax(n, 1)
+                turn_ax(n)
+            if filling:
+                group_ax(n)
+            if live(n - 3) and filling:
+                turn_normed(n - 3, 0)
+            if live(n - 3):
+                turn_normed(n - 3, 1)
+                gain_and_bias(n - 3)
+            if live(n) and not filling:
+                group_ax(n)
+            if live(n - 6):
+                add_bias(n - 6, 1, 1)
+            if live(n - 1) and not filling:
+                proj_matmul(n - 1, 0)
+            if live(n - 5):
+                add_bias(n - 5, 0, 0)
+            if live(n - 1) and not filling:
+                proj_matmul(n - 1, 1)
+            for c in W1_BANKS.get(n, ()):
+                turn_weight_rows(w1_raw[c // 2][:, 2 * (c % 2):2 * (c % 2) + 2, :], w1[c // 2][0], 2 * (c % 2))
+            if live(n - 5):
+                add_bias(n - 5, 0, 1)
+                ff_matmul(n - 5, 1, 1)
+                add_bias(n - 5, 1, 0)
+            if live(n - 1):
+                add_residual(n - 1, 0)
+                add_residual(n - 1, 1)
+            if n == 0:
+                quantize(*wo)
+            if n in W1_QUANT:
+                quantize(*w1[W1_QUANT.index(n)])
+            if live(n - 4):
+                m_q[n - 4] = quantize_pair(m_grouped[n - 4], "m")
+                ff_matmul(n - 4, 0, 0)
+                ff_matmul(n - 4, 0, 1)
+                ff_matmul(n - 4, 1, 0)
+            if live(n - 2):
+                rstd_of(n - 2)
+            if live(n):
+                ax_q[n] = quantize_pair(ax_grouped[n], "ax")
+            if live(n - 3) and vector_groups(n - 3):
+                group_m(n - 3)
+            if live(n - 2):
+                shift_of(n - 2)

@@ -22,16 +22,20 @@ PACK = 4
 BANK = 512
 TILES_PER_SEQ = T // P
 PAIRS = S * TILES_PER_SEQ // 2
-HEAD_PAIRS = 0
-TAIL_PAIRS = 2
-SCALAR_RELU_PAIRS = 1
-W1_BANKS = {1: (0, 1), 2: (2, 3)}
-W1_QUANT = (2, 3)
-GP_NORM_FROM = 0
-GP_NORM_TO = 14
-SHARED_RELU_PAIRS = 3
-FILL = 5
 F32_MAX = 3.4028234663852886e38
+
+SCALE_LEAD = 3
+TURN_LEAD = 1
+PROJ_LAG = 1
+STATS_LAG = 2
+NORM_LAG = 3
+QUANT_LAG = 4
+OUT_LAG = 5
+STEPS = PAIRS + OUT_LAG + 2
+FF1_TURNS = {1: (0,), 2: (1, 2), 3: (3,)}
+FF1_QUANT_STEPS = (3, 4)
+SCALAR_RELU_COLUMNS = 192
+SCALAR_RELU_FROM = (PAIRS - 4, PAIRS - 2)
 
 
 def tile_temporalatt_pb_t_kernel(tc, ax_bytes, ax_scale, features, wout_w, ln_g, ln_b, ff1_w, ff1_b, out):
@@ -45,23 +49,25 @@ def tile_temporalatt_pb_t_kernel(tc, ax_bytes, ax_scale, features, wout_w, ln_g,
         ident = keep.tile([P, P], F32, name="ident")
         make_identity(nc, ident[:])
 
-        ax_raw = {}
-        x_raw = {}
+        one = keep.tile([P, 1], F32, name="one")
+        nc.vector.memset(one[:], 1.0)
+        root = keep.tile([P, 1], F32, name="root")
+        nc.scalar.activation(out=root[:], in_=one[:], func=ACT.Sqrt)
+
+        ax_raw, x_raw = {}, {}
 
         def pair_rows(seq_rows, k):
             first = 2 * (k % 2)
-            return seq_rows.rearrange("(p j) d -> p j d", j=TILES_PER_SEQ)[:, first:first + 2, :]
+            return seq_rows.rearrange("(p i) d -> p i d", i=TILES_PER_SEQ)[:, first:first + 2, :]
 
         def load_ax(k):
-            codes_in = keep.tile([P, 2, D], U8, name="ax_bytes_%d" % k)
-            nc.sync.dma_start(out=codes_in[:], in_=pair_rows(ax_bytes[k // 2], k))
-            ax_raw[k] = codes_in
+            ax_raw[k] = keep.tile([P, 2, D], U8, name="ax_bytes_%d" % k)
+            nc.sync.dma_start(out=ax_raw[k][:], in_=pair_rows(ax_bytes[k // 2], k))
 
         def load_x(k):
             s = k // 2
-            rows = keep.tile([P, 2, D], BF16, name="x_%d" % k)
-            nc.sync.dma_start(out=rows[:], in_=pair_rows(features[s // N, :, s % N, :], k))
-            x_raw[k] = rows
+            x_raw[k] = keep.tile([P, 2, D], BF16, name="x_%d" % k)
+            nc.sync.dma_start(out=x_raw[k][:], in_=pair_rows(features[s // N, :, s % N, :], k))
 
         scale_col = keep.tile([P, PACK], F32, name="scale_col")
         nc.sync.dma_start(out=scale_col[:], in_=ax_scale.rearrange("a b (p t) -> p (a b t)", t=PACK))
@@ -74,23 +80,24 @@ def tile_temporalatt_pb_t_kernel(tc, ax_bytes, ax_scale, features, wout_w, ln_g,
             nc.sync.dma_start(out=rows[:], in_=wout_w.rearrange("(m t) k -> m t k", t=PACK)[:, 2 * half:2 * half + 2, :])
             wo_raw.append(rows)
         load_ax(1)
+        load_ax(2)
         load_x(0)
         w1_raw = []
         for half in range(2):
             rows = keep.tile([P, PACK, D], BF16, name="w1_raw_%d" % half)
             nc.sync.dma_start(out=rows[:], in_=ff1_w[half * BANK:(half + 1) * BANK, :].rearrange("(c m) k -> m c k", m=P))
             w1_raw.append(rows)
-            load_ax(2 + half)
-            load_x(1 + half)
+            load_ax(SCALE_LEAD + half)
+            load_x(PROJ_LAG + half)
         b_raw = keep.tile([P, PACK], BF16, name="b_raw")
         nc.sync.dma_start(out=b_raw[:], in_=ln_b.rearrange("(p t) -> p t", t=PACK))
-        load_ax(4)
+        load_ax(SCALE_LEAD + 2)
         bias_rows = keep.tile([P, F], BF16, name="bias_rows")
         nc.sync.dma_start(out=bias_rows[:], in_=ff1_b.partition_broadcast(P))
-        for k in range(3, PAIRS):
+        for k in range(SCALE_LEAD, PAIRS):
             load_x(k)
-            if k + 2 < PAIRS:
-                load_ax(k + 2)
+            if k + SCALE_LEAD < PAIRS:
+                load_ax(k + SCALE_LEAD)
 
         g_col = keep.tile([P, PACK], F32, name="g_col")
         nc.scalar.activation(out=g_col[:], in_=g_raw[:], func=ACT.Copy)
@@ -100,14 +107,15 @@ def tile_temporalatt_pb_t_kernel(tc, ax_bytes, ax_scale, features, wout_w, ln_g,
         for t in range(PACK):
             nc.tensor.transpose(scale_rows[:, :, t], scale_col[:, t:t + 1].to_broadcast([P, P]), ident[:])
 
-        def turn_weight_rows(raw, grouped, c0):
-            bank = psum.tile([P, 2, 2, P], F32, name="weight_bank", tag="acc", bufs=4)
+        def turn_rows(rows, bank):
             for c in range(2):
-                words = raw[:, c, :].bitcast(F32)
+                words = rows[:, c, :].bitcast(F32)
                 for u in range(2):
                     nc.tensor.transpose(bank[:, c, u, :], words[:, u::2], ident[:])
-            dst = grouped[:, c0 * P * PACK:(c0 + 2) * P * PACK].bitcast(F32)
-            nc.scalar.copy(out=dst.rearrange("p (c m u) -> p c m u", c=2, u=2), in_=bank[:].rearrange("p c u m -> p c m u"))
+
+        def group_rows(bank, grouped):
+            nc.scalar.copy(out=grouped.bitcast(F32).rearrange("p (c r u) -> p c r u", c=2, u=2),
+                           in_=bank[:].rearrange("p c u r -> p c r u"))
 
         def quantize(grouped, codes, scales):
             nc.vector.quantize_mx(out=codes[:].bitcast(FP8X4), scales=scales[:], in_=grouped[:])
@@ -118,193 +126,201 @@ def tile_temporalatt_pb_t_kernel(tc, ax_bytes, ax_scale, features, wout_w, ln_g,
             scales = keep.tile([P, BANK], U8, name=name + "_scales", align_bytes=64)
             return grouped, codes, scales
 
+        def group_weight_rows(rows, weight, half):
+            bank = psum.tile([P, 2, 2, P], F32, name="weight_bank", tag="acc", bufs=4)
+            turn_rows(rows, bank)
+            group_rows(bank, weight[0][:, half * 2 * P * PACK:(half + 1) * 2 * P * PACK])
+
         wo = weight_tiles("wo")
         w1 = [weight_tiles("w1_0"), weight_tiles("w1_1")]
 
-        ax_scaled, ax_bank, ax_grouped, ax_q = {}, {}, {}, {}
-        acc, resid, sums, sumsq, std, rstd, shift = {}, {}, {}, {}, {}, {}, {}
-        normed, z_banks, planes, m_grouped, m_q, staged = {}, {}, {}, {}, {}, {}
+        ax_scaled, ax_grouped, ax_q, acc, resid = {}, {}, {}, {}, {}
+        sums, sumsq, neg_mean, std, rstd = {}, {}, {}, {}, {}
+        normed, planes, m_grouped, m_q, staged = {}, {}, {}, {}, {}
 
-        def scale_ax(k, j):
-            if j == 0:
-                ax_scaled[k] = work.tile([P, 2, D], BF16, name="ax_scaled")
-            nc.vector.tensor_tensor(out=ax_scaled[k][:, j, :], in0=ax_raw[k][:, j, :].bitcast(FP8),
-                                    in1=scale_rows[:].rearrange("m p t -> m (p t)"), op=ALU.mult)
-
-        def turn_ax(k):
-            ax_bank[k] = psum.tile([P, 2, 2, P], F32, name="ax_bank")
+        def scale_ax(k):
+            ax_scaled[k] = work.tile([P, 2, D], BF16, name="ax_scaled", bufs=SCALE_LEAD + 2)
             for j in range(2):
-                words = ax_scaled[k][:, j, :].bitcast(F32)
-                for u in range(2):
-                    nc.tensor.transpose(ax_bank[k][:, j, u, :], words[:, u::2], ident[:])
+                nc.vector.tensor_tensor(out=ax_scaled[k][:, j, :], in0=ax_raw[k][:, j, :].bitcast(FP8),
+                                        in1=scale_rows[:].rearrange("m p t -> m (p t)"), op=ALU.mult)
 
         def group_ax(k):
+            bank = psum.tile([P, 2, 2, P], F32, name="ax_bank")
+            turn_rows(ax_scaled[k], bank)
             ax_grouped[k] = work.tile([P, 2 * P * PACK], BF16, name="ax_grouped", align_bytes=64)
-            nc.scalar.copy(out=ax_grouped[k][:].bitcast(F32).rearrange("p (j r u) -> p j r u", j=2, u=2),
-                           in_=ax_bank[k][:].rearrange("p j u r -> p j r u"))
+            group_rows(bank, ax_grouped[k][:])
 
         def quantize_pair(grouped, name):
-            codes = work.tile([P, 2 * P], U32, name=name + "_codes", align_bytes=64)
-            scales = work.tile([P, 2 * P], U8, name=name + "_scales", align_bytes=64)
+            codes = work.tile([P, 2 * P], U32, name=name + "_codes", align_bytes=64, bufs=5)
+            scales = work.tile([P, 2 * P], U8, name=name + "_scales", align_bytes=64, bufs=5)
             quantize(grouped, codes, scales)
             return codes, scales
 
         def matmul(key, operand, j, weight):
             codes, scales = operand
             acc[key] = psum.tile([P, BANK], F32, name="acc", bufs=4)
-            rows = slice(j * P, (j + 1) * P)
-            nc.tensor.matmul_mx(out=acc[key][:], lhsT=codes[:, rows].bitcast(FP8X4), lhsT_scale=scales[:, rows],
+            tokens = slice(j * P, (j + 1) * P)
+            nc.tensor.matmul_mx(out=acc[key][:], lhsT=codes[:, tokens].bitcast(FP8X4), lhsT_scale=scales[:, tokens],
                                 rhs=weight[1][:].bitcast(FP8X4), rhs_scale=weight[2][:], start=True, stop=True)
-
-        def add_residual(k, j):
-            if j == 0:
-                sums[k] = work.tile([P, 2], F32, name="sums", bufs=4)
-                sumsq[k] = work.tile([P, 2], F32, name="sumsq", bufs=4)
-            resid[k, j] = work.tile([P, D], F32, name="resid", bufs=8)
-            nc.vector.scalar_tensor_tensor(
-                out=resid[k, j][:].rearrange("p (t m) -> p t m", t=PACK),
-                in0=acc["proj", k, j][:].rearrange("p (t m) -> p t m", t=PACK), scalar=1.0,
-                in1=x_raw[k][:, j, :].rearrange("p (m t) -> p t m", t=PACK),
-                op0=ALU.mult, op1=ALU.add, accum_out=sums[k][:, j:j + 1])
-
-        def square_sum(k, j):
-            squares = work.tile([P, D], BF16, name="squares", bufs=2)
-            nc.scalar.activation(out=squares[:], in_=resid[k, j][:], func=ACT.Square, scale=-float(D),
-                                 bias=sums[k][:, j:j + 1], accum_out=sumsq[k][:, j:j + 1])
-
-        def std_of(k):
-            std[k] = work.tile([P, 2], F32, name="std")
-            nc.scalar.activation(out=std[k][:], in_=sumsq[k][:], func=ACT.Sqrt, scale=1.0 / D ** 3, bias=EPS)
-
-        def rstd_of(k):
-            rstd[k] = work.tile([P, 2], F32, name="rstd")
-            nc.vector.reciprocal(out=rstd[k][:], in_=std[k][:])
-
-        def shift_of(k):
-            shift[k] = work.tile([P, 2], F32, name="shift")
-            nc.vector.scalar_tensor_tensor(out=shift[k][:], in0=sums[k][:], scalar=-1.0 / D, in1=rstd[k][:],
-                                           op0=ALU.mult, op1=ALU.mult)
-
-        def normalise(k):
-            for j in range(2):
-                normed[k, j] = work.tile([P, D], F32, name="normed", bufs=4)
-                if GP_NORM_FROM <= k < GP_NORM_TO:
-                    nc.gpsimd.tensor_scalar(out=normed[k, j][:], in0=resid[k, j][:], scalar1=rstd[k][:, j:j + 1],
-                                            scalar2=shift[k][:, j:j + 1], op0=ALU.mult, op1=ALU.add)
-                else:
-                    nc.scalar.activation(out=normed[k, j][:], in_=resid[k, j][:], func=ACT.Identity,
-                                         scale=rstd[k][:, j:j + 1], bias=shift[k][:, j:j + 1])
-
-        def turn_normed(k, j):
-            if j == 0:
-                for h in range(2):
-                    z_banks[k, h] = psum.tile([P, 2, 2 * P], F32, name="z_bank", bufs=2)
-            for t in range(PACK):
-                nc.tensor.transpose(z_banks[k, t // 2][:, t % 2, j * P:(j + 1) * P], normed[k, j][:, t * P:(t + 1) * P], ident[:])
-
-        def gain_and_bias(k):
-            planes[k] = work.tile([P, PACK, 2 * P], BF16, name="planes", bufs=2)
-            for t in range(PACK):
-                nc.scalar.activation(out=planes[k][:, t, :], in_=z_banks[k, t // 2][:, t % 2, :], func=ACT.Identity,
-                                     scale=g_col[:, t:t + 1], bias=b_col[:, t:t + 1])
-
-        def vector_groups(k):
-            return k < HEAD_PAIRS or k >= PAIRS - TAIL_PAIRS
-
-        def group_m(k):
-            m_grouped[k] = work.tile([P, 2 * P * PACK], BF16, name="m_grouped", align_bytes=64)
-            copy = nc.vector.tensor_copy if vector_groups(k) else nc.scalar.copy
-            copy(out=m_grouped[k][:].rearrange("p (c i t) -> p c t i", i=4, t=PACK),
-                 in_=planes[k][:].rearrange("p t (c i) -> p c t i", i=4))
-
-        def add_bias(k, j, half):
-            if half == 0:
-                staged[k, j] = work.tile([P, F], F32, name="staged", bufs=6)
-            cols = slice(half * BANK, (half + 1) * BANK)
-            nc.vector.tensor_tensor(out=staged[k, j][:, cols], in0=acc["ff", k, j, half][:], in1=bias_rows[:, cols], op=ALU.add)
-            rows = out[k // 2].rearrange("(p j) f -> p j f", j=TILES_PER_SEQ)[:, 2 * (k % 2) + j, :]
-            if k >= PAIRS - SCALAR_RELU_PAIRS or (j == 0 and k >= PAIRS - SHARED_RELU_PAIRS):
-                nc.scalar.activation(out=staged[k, j][:, cols], in_=staged[k, j][:, cols], func=ACT.Relu)
-                nc.sync.dma_start(out=rows[:, cols], in_=staged[k, j][:, cols])
-            elif half == 1:
-                nc.gpsimd.tensor_scalar(out=staged[k, j][:], in0=staged[k, j][:], scalar1=F32_MAX, scalar2=0.0,
-                                        op0=ALU.min, op1=ALU.max)
-                nc.sync.dma_start(out=rows, in_=staged[k, j][:])
-
-        def ff_matmul(k, j, half):
-            matmul(("ff", k, j, half), m_q[k], j, w1[half])
 
         def proj_matmul(k, j):
             matmul(("proj", k, j), ax_q[k], j, wo)
 
+        def ff_matmul(k, j, half):
+            matmul(("ff", k, j, half), m_q[k], j, w1[half])
+
+        def add_residual(k):
+            sums[k] = work.tile([P, 2], F32, name="sums", bufs=4)
+            for j in range(2):
+                resid[k, j] = work.tile([P, D], F32, name="resid", bufs=8)
+                nc.vector.scalar_tensor_tensor(
+                    out=resid[k, j][:].rearrange("p (t m) -> p t m", t=PACK),
+                    in0=acc["proj", k, j][:].rearrange("p (t m) -> p t m", t=PACK), scalar=1.0,
+                    in1=x_raw[k][:, j, :].rearrange("p (m t) -> p t m", t=PACK),
+                    op0=ALU.mult, op1=ALU.add, accum_out=sums[k][:, j:j + 1])
+
+        def sum_squares(k):
+            sumsq[k] = work.tile([P, 2], F32, name="sumsq", bufs=4)
+            for j in range(2):
+                squares = work.tile([P, D], BF16, name="squares", bufs=2)
+                nc.scalar.activation(out=squares[:], in_=resid[k, j][:], func=ACT.Square, scale=-float(D),
+                                     bias=sums[k][:, j:j + 1], accum_out=sumsq[k][:, j:j + 1])
+
+        def mean_and_std(k):
+            neg_mean[k] = work.tile([P, 2], F32, name="neg_mean")
+            nc.scalar.activation(out=neg_mean[k][:], in_=sums[k][:], func=ACT.Copy, scale=-1.0 / D)
+            std[k] = work.tile([P, 2], F32, name="std")
+            nc.scalar.activation(out=std[k][:], in_=sumsq[k][:], func=ACT.Sqrt, scale=1.0 / D ** 3, bias=EPS)
+
+        def invert_std(k):
+            rstd[k] = work.tile([P, 2], F32, name="rstd")
+            nc.vector.reciprocal(out=rstd[k][:], in_=std[k][:])
+
+        def normalise(k):
+            for j in range(2):
+                normed[k, j] = work.tile([P, D], F32, name="normed", bufs=6)
+                nc.gpsimd.tensor_scalar(out=normed[k, j][:], in0=resid[k, j][:], scalar1=neg_mean[k][:, j:j + 1],
+                                        scalar2=rstd[k][:, j:j + 1], op0=ALU.add, op1=ALU.mult)
+
+        def gain_and_bias(k):
+            banks = [psum.tile([P, 2, 2 * P], F32, name="plane_bank", bufs=2) for h in range(2)]
+            for j in range(2):
+                for t in range(PACK):
+                    nc.tensor.transpose(banks[t // 2][:, t % 2, j * P:(j + 1) * P], normed[k, j][:, t * P:(t + 1) * P], ident[:])
+            planes[k] = work.tile([P, PACK, 2 * P], BF16, name="planes")
+            for t in range(PACK):
+                nc.scalar.activation(out=planes[k][:, t, :], in_=banks[t // 2][:, t % 2, :], func=ACT.Identity,
+                                     scale=g_col[:, t:t + 1], bias=b_col[:, t:t + 1])
+
+        def group_m(k, copy):
+            m_grouped[k] = work.tile([P, 2 * P * PACK], BF16, name="m_grouped", align_bytes=64)
+            copy(out=m_grouped[k][:].rearrange("p (c i t) -> p c t i", i=4, t=PACK),
+                 in_=planes[k][:].rearrange("p t (c i) -> p c t i", i=4))
+
+        def relu_engine(k, j):
+            if k >= SCALAR_RELU_FROM[j]:
+                return "scalar"
+            if j == 0 and k + OUT_LAG + SCALE_LEAD >= PAIRS:
+                return "vector"
+            return "gpsimd"
+
+        def store(k, j, cols):
+            nc.sync.dma_start(out=pair_rows(out[k // 2], k)[:, j, cols], in_=staged[k, j][:, cols])
+
+        def scalar_relu(k, j, cols):
+            nc.scalar.activation(out=staged[k, j][:, cols], in_=staged[k, j][:, cols], func=ACT.Relu)
+
+        def add_bias(k, j, half):
+            if half == 0:
+                staged[k, j] = work.tile([P, F], F32, name="staged", bufs=8)
+            cols = slice(half * BANK, (half + 1) * BANK)
+            nc.vector.tensor_tensor(out=staged[k, j][:, cols], in0=acc["ff", k, j, half][:], in1=bias_rows[:, cols], op=ALU.add)
+            if relu_engine(k, j) == "scalar":
+                scalar_relu(k, j, cols)
+                store(k, j, cols)
+            elif relu_engine(k, j) == "gpsimd" and half == 1:
+                own = slice(SCALAR_RELU_COLUMNS if j == 1 else 0, F)
+                nc.gpsimd.tensor_scalar(out=staged[k, j][:, own], in0=staged[k, j][:, own], scalar1=F32_MAX, scalar2=0.0,
+                                        op0=ALU.min, op1=ALU.max)
+                store(k, j, slice(0, F))
+
+        def vector_relu(k, j):
+            nc.vector.tensor_scalar(out=staged[k, j][:], in0=staged[k, j][:], scalar1=0.0, scalar2=None, op0=ALU.max)
+            store(k, j, slice(0, F))
+
         def live(k):
             return 0 <= k < PAIRS
 
-        turn_weight_rows(wo_raw[0], wo[0], 0)
-        turn_weight_rows(wo_raw[1], wo[0], 2)
+        for half in range(2):
+            group_weight_rows(wo_raw[half], wo, half)
+        for k in range(SCALE_LEAD):
+            scale_ax(k)
+        for k in range(TURN_LEAD):
+            group_ax(k)
+        quantize(*wo)
+        for k in range(TURN_LEAD):
+            ax_q[k] = quantize_pair(ax_grouped[k], "ax")
 
-        for n in range(PAIRS + 7):
-            filling = n < FILL
-            if n == 2:
+        for n in range(STEPS):
+            scaling, turning, projecting = n + SCALE_LEAD, n + TURN_LEAD, n - PROJ_LAG
+            measuring, norming, quantising = n - STATS_LAG, n - NORM_LAG, n - QUANT_LAG
+            leaving, closing = n - OUT_LAG, n - OUT_LAG - 1
+            banks_free = n < OUT_LAG
+            last_group = quantising == PAIRS - 1
+
+            if n == NORM_LAG - 1:
                 nc.scalar.activation(out=b_col[:], in_=b_raw[:], func=ACT.Copy)
-            if live(n - 1) and filling:
-                proj_matmul(n - 1, 0)
-                proj_matmul(n - 1, 1)
-            if live(n - 2):
-                square_sum(n - 2, 0)
-                square_sum(n - 2, 1)
-            if live(n - 4) and not vector_groups(n - 4):
-                group_m(n - 4)
-            if live(n - 2):
-                std_of(n - 2)
-            if live(n - 3):
-                normalise(n - 3)
-            if live(n - 3) and not filling:
-                turn_normed(n - 3, 0)
-            if live(n):
-                scale_ax(n, 0)
-                scale_ax(n, 1)
-                turn_ax(n)
-            if filling:
-                group_ax(n)
-            if live(n - 3) and filling:
-                turn_normed(n - 3, 0)
-            if live(n - 3):
-                turn_normed(n - 3, 1)
-                gain_and_bias(n - 3)
-            if live(n) and not filling:
-                group_ax(n)
-            if live(n - 6):
-                add_bias(n - 6, 1, 1)
-            if live(n - 1) and not filling:
-                proj_matmul(n - 1, 0)
-            if live(n - 5):
-                add_bias(n - 5, 0, 0)
-            if live(n - 1) and not filling:
-                proj_matmul(n - 1, 1)
-            for c in W1_BANKS.get(n, ()):
-                turn_weight_rows(w1_raw[c // 2][:, 2 * (c % 2):2 * (c % 2) + 2, :], w1[c // 2][0], 2 * (c % 2))
-            if live(n - 5):
-                add_bias(n - 5, 0, 1)
-                ff_matmul(n - 5, 1, 1)
-                add_bias(n - 5, 1, 0)
-            if live(n - 1):
-                add_residual(n - 1, 0)
-                add_residual(n - 1, 1)
-            if n == 0:
-                quantize(*wo)
-            if n in W1_QUANT:
-                quantize(*w1[W1_QUANT.index(n)])
-            if live(n - 4):
-                m_q[n - 4] = quantize_pair(m_grouped[n - 4], "m")
-                ff_matmul(n - 4, 0, 0)
-                ff_matmul(n - 4, 0, 1)
-                ff_matmul(n - 4, 1, 0)
-            if live(n - 2):
-                rstd_of(n - 2)
-            if live(n):
-                ax_q[n] = quantize_pair(ax_grouped[n], "ax")
-            if live(n - 3) and vector_groups(n - 3):
-                group_m(n - 3)
-            if live(n - 2):
-                shift_of(n - 2)
+            if live(projecting) and banks_free:
+                proj_matmul(projecting, 0)
+                proj_matmul(projecting, 1)
+            if live(measuring):
+                sum_squares(measuring)
+            if live(norming):
+                normalise(norming)
+            if live(closing) and relu_engine(closing, 1) == "gpsimd":
+                scalar_relu(closing, 1, slice(0, SCALAR_RELU_COLUMNS))
+            if live(quantising) and not last_group:
+                group_m(quantising, nc.scalar.copy)
+            if live(measuring):
+                mean_and_std(measuring)
+            if live(scaling):
+                scale_ax(scaling)
+            if live(turning):
+                group_ax(turning)
+
+            if live(closing):
+                add_bias(closing, 1, 1)
+            if live(projecting) and not banks_free:
+                proj_matmul(projecting, 0)
+            if live(leaving):
+                add_bias(leaving, 0, 0)
+            if live(projecting) and not banks_free:
+                proj_matmul(projecting, 1)
+            if live(norming):
+                gain_and_bias(norming)
+            for c in FF1_TURNS.get(n, ()):
+                group_weight_rows(w1_raw[c // 2][:, 2 * (c % 2):2 * (c % 2) + 2, :], w1[c // 2], c % 2)
+            if live(leaving):
+                add_bias(leaving, 0, 1)
+                ff_matmul(leaving, 1, 1)
+            if last_group:
+                group_m(quantising, nc.vector.tensor_copy)
+            if live(leaving):
+                add_bias(leaving, 1, 0)
+            if live(projecting):
+                add_residual(projecting)
+
+            if n in FF1_QUANT_STEPS:
+                quantize(*w1[FF1_QUANT_STEPS.index(n)])
+            if live(quantising):
+                m_q[quantising] = quantize_pair(m_grouped[quantising], "m")
+            if live(turning):
+                ax_q[turning] = quantize_pair(ax_grouped[turning], "ax")
+            if live(quantising):
+                ff_matmul(quantising, 0, 0)
+                ff_matmul(quantising, 0, 1)
+                ff_matmul(quantising, 1, 0)
+            if live(leaving) and relu_engine(leaving, 0) == "vector":
+                vector_relu(leaving, 0)
+            if live(measuring):
+                invert_std(measuring)

from contextlib import ExitStack

import concourse.mybir as mybir
from concourse.masks import make_identity

B, T, N, D, F = 2, 512, 4, 512, 1024
S = B * N
EPS = 1e-5
FLOPS = 2 * S * T * D * (D + F)

F32 = mybir.dt.float32
BF16 = mybir.dt.bfloat16
U32 = mybir.dt.uint32
U8 = mybir.dt.uint8
FP8 = mybir.dt.float8_e4m3fn
FP8X4 = mybir.dt.float8_e4m3fn_x4
ALU = mybir.AluOpType
ACT = mybir.ActivationFunctionType

P = 128
PACK = 4
BANK = 512
TILES_PER_SEQ = T // P
PAIRS = S * TILES_PER_SEQ // 2
F32_MAX = 3.4028234663852886e38

SCALE_LEAD = 3
TURN_LEAD = 1
PROJ_LAG = 1
STATS_LAG = 2
NORM_LAG = 3
QUANT_LAG = 4
OUT_LAG = 5
STEPS = PAIRS + OUT_LAG + 2
FF1_TURNS = {1: (0,), 2: (1, 2), 3: (3,)}
FF1_QUANT_STEPS = (3, 4)
SCALAR_RELU_COLUMNS = 192
SCALAR_RELU_FROM = (PAIRS - 4, PAIRS - 2)


def tile_temporalatt_pb_t_kernel(tc, ax_bytes, ax_scale, features, wout_w, ln_g, ln_b, ff1_w, ff1_b, out):
    nc = tc.nc
    with ExitStack() as ctx:
        keep = ctx.enter_context(tc.tile_pool(name="keep", bufs=1))
        work = ctx.enter_context(tc.tile_pool(name="work", bufs=3))
        psum = ctx.enter_context(tc.psum_pool(name="psum", bufs=1))
        ctx.enter_context(tc.manual_schedule())

        ident = keep.tile([P, P], F32, name="ident")
        make_identity(nc, ident[:])

        one = keep.tile([P, 1], F32, name="one")
        nc.vector.memset(one[:], 1.0)
        root = keep.tile([P, 1], F32, name="root")
        nc.scalar.activation(out=root[:], in_=one[:], func=ACT.Sqrt)

        ax_raw, x_raw = {}, {}

        def pair_rows(seq_rows, k):
            first = 2 * (k % 2)
            return seq_rows.rearrange("(p i) d -> p i d", i=TILES_PER_SEQ)[:, first:first + 2, :]

        def load_ax(k):
            ax_raw[k] = keep.tile([P, 2, D], U8, name="ax_bytes_%d" % k)
            nc.sync.dma_start(out=ax_raw[k][:], in_=pair_rows(ax_bytes[k // 2], k))

        def load_x(k):
            s = k // 2
            x_raw[k] = keep.tile([P, 2, D], BF16, name="x_%d" % k)
            nc.sync.dma_start(out=x_raw[k][:], in_=pair_rows(features[s // N, :, s % N, :], k))

        scale_col = keep.tile([P, PACK], F32, name="scale_col")
        nc.sync.dma_start(out=scale_col[:], in_=ax_scale.rearrange("a b (p t) -> p (a b t)", t=PACK))
        g_raw = keep.tile([P, PACK], BF16, name="g_raw")
        nc.sync.dma_start(out=g_raw[:], in_=ln_g.rearrange("(p t) -> p t", t=PACK))
        load_ax(0)
        wo_raw = []
        for half in range(2):
            rows = keep.tile([P, 2, D], BF16, name="wo_raw_%d" % half)
            nc.sync.dma_start(out=rows[:], in_=wout_w.rearrange("(m t) k -> m t k", t=PACK)[:, 2 * half:2 * half + 2, :])
            wo_raw.append(rows)
        load_ax(1)
        load_ax(2)
        load_x(0)
        w1_raw = []
        for half in range(2):
            rows = keep.tile([P, PACK, D], BF16, name="w1_raw_%d" % half)
            nc.sync.dma_start(out=rows[:], in_=ff1_w[half * BANK:(half + 1) * BANK, :].rearrange("(c m) k -> m c k", m=P))
            w1_raw.append(rows)
            load_ax(SCALE_LEAD + half)
            load_x(PROJ_LAG + half)
        b_raw = keep.tile([P, PACK], BF16, name="b_raw")
        nc.sync.dma_start(out=b_raw[:], in_=ln_b.rearrange("(p t) -> p t", t=PACK))
        load_ax(SCALE_LEAD + 2)
        bias_rows = keep.tile([P, F], BF16, name="bias_rows")
        nc.sync.dma_start(out=bias_rows[:], in_=ff1_b.partition_broadcast(P))
        for k in range(SCALE_LEAD, PAIRS):
            load_x(k)
            if k + SCALE_LEAD < PAIRS:
                load_ax(k + SCALE_LEAD)

        g_col = keep.tile([P, PACK], F32, name="g_col")
        nc.scalar.activation(out=g_col[:], in_=g_raw[:], func=ACT.Copy)
        b_col = keep.tile([P, PACK], F32, name="b_col")

        scale_rows = psum.tile([P, P, PACK], F32, name="scale_rows")
        for t in range(PACK):
            nc.tensor.transpose(scale_rows[:, :, t], scale_col[:, t:t + 1].to_broadcast([P, P]), ident[:])

        def turn_rows(rows, bank):
            for c in range(2):
                words = rows[:, c, :].bitcast(F32)
                for u in range(2):
                    nc.tensor.transpose(bank[:, c, u, :], words[:, u::2], ident[:])

        def group_rows(bank, grouped):
            nc.scalar.copy(out=grouped.bitcast(F32).rearrange("p (c r u) -> p c r u", c=2, u=2),
                           in_=bank[:].rearrange("p c u r -> p c r u"))

        def quantize(grouped, codes, scales):
            nc.vector.quantize_mx(out=codes[:].bitcast(FP8X4), scales=scales[:], in_=grouped[:])

        def weight_tiles(name):
            grouped = keep.tile([P, BANK * PACK], BF16, name=name + "_grouped", align_bytes=64)
            codes = keep.tile([P, BANK], U32, name=name + "_codes", align_bytes=64)
            scales = keep.tile([P, BANK], U8, name=name + "_scales", align_bytes=64)
            return grouped, codes, scales

        def group_weight_rows(rows, weight, half):
            bank = psum.tile([P, 2, 2, P], F32, name="weight_bank", tag="acc", bufs=4)
            turn_rows(rows, bank)
            group_rows(bank, weight[0][:, half * 2 * P * PACK:(half + 1) * 2 * P * PACK])

        wo = weight_tiles("wo")
        w1 = [weight_tiles("w1_0"), weight_tiles("w1_1")]

        ax_scaled, ax_grouped, ax_q, acc, resid = {}, {}, {}, {}, {}
        sums, sumsq, neg_mean, std, rstd = {}, {}, {}, {}, {}
        normed, planes, m_grouped, m_q, staged = {}, {}, {}, {}, {}

        def scale_ax(k):
            ax_scaled[k] = work.tile([P, 2, D], BF16, name="ax_scaled", bufs=SCALE_LEAD + 2)
            for j in range(2):
                nc.vector.tensor_tensor(out=ax_scaled[k][:, j, :], in0=ax_raw[k][:, j, :].bitcast(FP8),
                                        in1=scale_rows[:].rearrange("m p t -> m (p t)"), op=ALU.mult)

        def group_ax(k):
            bank = psum.tile([P, 2, 2, P], F32, name="ax_bank")
            turn_rows(ax_scaled[k], bank)
            ax_grouped[k] = work.tile([P, 2 * P * PACK], BF16, name="ax_grouped", align_bytes=64)
            group_rows(bank, ax_grouped[k][:])

        def quantize_pair(grouped, name):
            codes = work.tile([P, 2 * P], U32, name=name + "_codes", align_bytes=64, bufs=5)
            scales = work.tile([P, 2 * P], U8, name=name + "_scales", align_bytes=64, bufs=5)
            quantize(grouped, codes, scales)
            return codes, scales

        def matmul(key, operand, j, weight):
            codes, scales = operand
            acc[key] = psum.tile([P, BANK], F32, name="acc", bufs=4)
            tokens = slice(j * P, (j + 1) * P)
            nc.tensor.matmul_mx(out=acc[key][:], lhsT=codes[:, tokens].bitcast(FP8X4), lhsT_scale=scales[:, tokens],
                                rhs=weight[1][:].bitcast(FP8X4), rhs_scale=weight[2][:], start=True, stop=True)

        def proj_matmul(k, j):
            matmul(("proj", k, j), ax_q[k], j, wo)

        def ff_matmul(k, j, half):
            matmul(("ff", k, j, half), m_q[k], j, w1[half])

        def add_residual(k):
            sums[k] = work.tile([P, 2], F32, name="sums", bufs=4)
            for j in range(2):
                resid[k, j] = work.tile([P, D], F32, name="resid", bufs=8)
                nc.vector.scalar_tensor_tensor(
                    out=resid[k, j][:].rearrange("p (t m) -> p t m", t=PACK),
                    in0=acc["proj", k, j][:].rearrange("p (t m) -> p t m", t=PACK), scalar=1.0,
                    in1=x_raw[k][:, j, :].rearrange("p (m t) -> p t m", t=PACK),
                    op0=ALU.mult, op1=ALU.add, accum_out=sums[k][:, j:j + 1])

        def sum_squares(k):
            sumsq[k] = work.tile([P, 2], F32, name="sumsq", bufs=4)
            for j in range(2):
                squares = work.tile([P, D], BF16, name="squares", bufs=2)
                nc.scalar.activation(out=squares[:], in_=resid[k, j][:], func=ACT.Square, scale=-float(D),
                                     bias=sums[k][:, j:j + 1], accum_out=sumsq[k][:, j:j + 1])

        def mean_and_std(k):
            neg_mean[k] = work.tile([P, 2], F32, name="neg_mean")
            nc.scalar.activation(out=neg_mean[k][:], in_=sums[k][:], func=ACT.Copy, scale=-1.0 / D)
            std[k] = work.tile([P, 2], F32, name="std")
            nc.scalar.activation(out=std[k][:], in_=sumsq[k][:], func=ACT.Sqrt, scale=1.0 / D ** 3, bias=EPS)

        def invert_std(k):
            rstd[k] = work.tile([P, 2], F32, name="rstd")
            nc.vector.reciprocal(out=rstd[k][:], in_=std[k][:])

        def normalise(k):
            for j in range(2):
                normed[k, j] = work.tile([P, D], F32, name="normed", bufs=6)
                nc.gpsimd.tensor_scalar(out=normed[k, j][:], in0=resid[k, j][:], scalar1=neg_mean[k][:, j:j + 1],
                                        scalar2=rstd[k][:, j:j + 1], op0=ALU.add, op1=ALU.mult)

        def gain_and_bias(k):
            banks = [psum.tile([P, 2, 2 * P], F32, name="plane_bank", bufs=2) for h in range(2)]
            for j in range(2):
                for t in range(PACK):
                    nc.tensor.transpose(banks[t // 2][:, t % 2, j * P:(j + 1) * P], normed[k, j][:, t * P:(t + 1) * P], ident[:])
            planes[k] = work.tile([P, PACK, 2 * P], BF16, name="planes")
            for t in range(PACK):
                nc.scalar.activation(out=planes[k][:, t, :], in_=banks[t // 2][:, t % 2, :], func=ACT.Identity,
                                     scale=g_col[:, t:t + 1], bias=b_col[:, t:t + 1])

        def group_m(k, copy):
            m_grouped[k] = work.tile([P, 2 * P * PACK], BF16, name="m_grouped", align_bytes=64)
            copy(out=m_grouped[k][:].rearrange("p (c i t) -> p c t i", i=4, t=PACK),
                 in_=planes[k][:].rearrange("p t (c i) -> p c t i", i=4))

        def relu_engine(k, j):
            if k >= SCALAR_RELU_FROM[j]:
                return "scalar"
            if j == 0 and k + OUT_LAG + SCALE_LEAD >= PAIRS:
                return "vector"
            return "gpsimd"

        def store(k, j, cols):
            nc.sync.dma_start(out=pair_rows(out[k // 2], k)[:, j, cols], in_=staged[k, j][:, cols])

        def scalar_relu(k, j, cols):
            nc.scalar.activation(out=staged[k, j][:, cols], in_=staged[k, j][:, cols], func=ACT.Relu)

        def add_bias(k, j, half):
            if half == 0:
                staged[k, j] = work.tile([P, F], F32, name="staged", bufs=8)
            cols = slice(half * BANK, (half + 1) * BANK)
            nc.vector.tensor_tensor(out=staged[k, j][:, cols], in0=acc["ff", k, j, half][:], in1=bias_rows[:, cols], op=ALU.add)
            if relu_engine(k, j) == "scalar":
                scalar_relu(k, j, cols)
                store(k, j, cols)
            elif relu_engine(k, j) == "gpsimd" and half == 1:
                own = slice(SCALAR_RELU_COLUMNS if j == 1 else 0, F)
                nc.gpsimd.tensor_scalar(out=staged[k, j][:, own], in0=staged[k, j][:, own], scalar1=F32_MAX, scalar2=0.0,
                                        op0=ALU.min, op1=ALU.max)
                store(k, j, slice(0, F))

        def vector_relu(k, j):
            nc.vector.tensor_scalar(out=staged[k, j][:], in0=staged[k, j][:], scalar1=0.0, scalar2=None, op0=ALU.max)
            store(k, j, slice(0, F))

        def live(k):
            return 0 <= k < PAIRS

        for half in range(2):
            group_weight_rows(wo_raw[half], wo, half)
        for k in range(SCALE_LEAD):
            scale_ax(k)
        for k in range(TURN_LEAD):
            group_ax(k)
        quantize(*wo)
        for k in range(TURN_LEAD):
            ax_q[k] = quantize_pair(ax_grouped[k], "ax")

        for n in range(STEPS):
            scaling, turning, projecting = n + SCALE_LEAD, n + TURN_LEAD, n - PROJ_LAG
            measuring, norming, quantising = n - STATS_LAG, n - NORM_LAG, n - QUANT_LAG
            leaving, closing = n - OUT_LAG, n - OUT_LAG - 1
            banks_free = n < OUT_LAG
            last_group = quantising == PAIRS - 1

            if n == NORM_LAG - 1:
                nc.scalar.activation(out=b_col[:], in_=b_raw[:], func=ACT.Copy)
            if live(projecting) and banks_free:
                proj_matmul(projecting, 0)
                proj_matmul(projecting, 1)
            if live(measuring):
                sum_squares(measuring)
            if live(norming):
                normalise(norming)
            if live(closing) and relu_engine(closing, 1) == "gpsimd":
                scalar_relu(closing, 1, slice(0, SCALAR_RELU_COLUMNS))
            if live(quantising) and not last_group:
                group_m(quantising, nc.scalar.copy)
            if live(measuring):
                mean_and_std(measuring)
            if live(scaling):
                scale_ax(scaling)
            if live(turning):
                group_ax(turning)

            if live(closing):
                add_bias(closing, 1, 1)
            if live(projecting) and not banks_free:
                proj_matmul(projecting, 0)
            if live(leaving):
                add_bias(leaving, 0, 0)
            if live(projecting) and not banks_free:
                proj_matmul(projecting, 1)
            if live(norming):
                gain_and_bias(norming)
            for c in FF1_TURNS.get(n, ()):
                group_weight_rows(w1_raw[c // 2][:, 2 * (c % 2):2 * (c % 2) + 2, :], w1[c // 2], c % 2)
            if live(leaving):
                add_bias(leaving, 0, 1)
                ff_matmul(leaving, 1, 1)
            if last_group:
                group_m(quantising, nc.vector.tensor_copy)
            if live(leaving):
                add_bias(leaving, 1, 0)
            if live(projecting):
                add_residual(projecting)

            if n in FF1_QUANT_STEPS:
                quantize(*w1[FF1_QUANT_STEPS.index(n)])
            if live(quantising):
                m_q[quantising] = quantize_pair(m_grouped[quantising], "m")
            if live(turning):
                ax_q[turning] = quantize_pair(ax_grouped[turning], "ax")
            if live(quantising):
                ff_matmul(quantising, 0, 0)
                ff_matmul(quantising, 0, 1)
                ff_matmul(quantising, 1, 0)
            if live(leaving) and relu_engine(leaving, 0) == "vector":
                vector_relu(leaving, 0)
            if live(measuring):
                invert_std(measuring)
